import numpy as np
import ml_dtypes


def mxq(x, axis, fmt="e4m3"):
    dtype, down = {"e4m3": (ml_dtypes.float8_e4m3fn, 7), "e5m2": (ml_dtypes.float8_e5m2, 14)}[fmt]
    v = np.moveaxis(np.asarray(x, np.float32).astype(ml_dtypes.bfloat16).astype(np.float64), axis, -1)
    blocks = v.reshape(v.shape[:-1] + (-1, 32))
    amax = np.abs(blocks).max(-1, keepdims=True)
    byte = np.maximum(np.where(amax > 0, np.frexp(amax)[1] - 1 + 127, 0) - down, 1)
    scale = np.exp2(byte - 127.0)
    codes = (blocks / scale).astype(np.float32).astype(dtype).astype(np.float64)
    return np.moveaxis((codes * scale).reshape(v.shape), -1, axis)


WIDE = False


def mx_kscale(k):
    if not WIDE:
        return np.ones(k)
    levels = np.array([10, -10, 5, -5, 0])
    a = np.random.permutation(np.resize(levels, k // 512 * 4)).reshape(k // 512, 4)
    idx = np.arange(k)
    return np.exp2(a[idx // 512, idx % 128 // 32])


BF16 = ml_dtypes.bfloat16


def bf(x):
    return np.asarray(x, np.float32).astype(BF16)


def f64(x):
    return np.asarray(x).astype(np.float64)


E2M1 = np.array([0.0, 0.5, 1.0, 1.5, 2.0, 3.0, 4.0, 6.0, -0.0, -0.5, -1.0, -1.5, -2.0, -3.0, -4.0, -6.0])


def pack_weight(w, fmt):
    k, n = w.shape
    w = f64(bf(w)).reshape(k // 32, 32, n)
    amax = np.abs(w).max(1)
    if fmt == "e4m3":
        byte = np.frexp(amax)[1] - 1 + 127 - 7
    else:
        mant, ex = np.frexp(amax / 6.0)
        byte = np.where(mant > 0.5, ex, ex - 1) + 127
    byte = np.clip(np.where(amax > 0, byte, 1), 1, 254)
    scaled = (w * np.exp2(127.0 - byte)[:, None, :]).reshape(k, n).astype(np.float32)
    by_word = np.ascontiguousarray(scaled.reshape(k // 512, 128, 4, n).transpose(0, 1, 3, 2))
    if fmt == "e4m3":
        words = by_word.astype(ml_dtypes.float8_e4m3fn).view(np.uint8)
    else:
        c = by_word.astype(ml_dtypes.float4_e2m1fn).view(np.uint8) & 0xF
        words = c[..., 0::2] | (c[..., 1::2] << 4)
    return np.ascontiguousarray(words), np.ascontiguousarray(byte.astype(np.uint8).reshape(k // 512, 16, n))


def unpack_weight(words, scales, fmt):
    g, p, n, _ = words.shape
    if fmt == "e4m3":
        vals = np.ascontiguousarray(words).view(ml_dtypes.float8_e4m3fn).astype(np.float64)
    else:
        nib = np.empty((g, p, n, 4), np.uint8)
        nib[..., 0::2] = words & 0xF
        nib[..., 1::2] = words >> 4
        vals = E2M1[nib]
    vals = vals * np.repeat(np.exp2(scales.astype(np.float64) - 127.0), 8, axis=1)[..., None]
    return vals.transpose(0, 1, 3, 2).reshape(g * 512, n)


B, E, D = 128, 16384, 512
FMT = "e4m3"


def hard_sigmoid(z):
    return np.clip(z / 6.0 + 0.5, 0.0, 1.0)


def setup_inputs():
    s = mx_kscale(E)
    t = mx_kscale(D)
    x = bf(np.random.standard_normal((B, E)) * s)
    state_x = bf(np.random.standard_normal((B, E)) * s)
    time_mix_r = bf(np.random.uniform(0.0, 1.0, (1, E)))
    w_r = np.random.standard_normal((D, E)) * 3.5 / np.sqrt(E) / s[None, :]
    wr_words, wr_scales = pack_weight(np.ascontiguousarray(w_r.T), FMT)
    wkv_num = bf((0.5 + 0.5 * np.random.standard_normal((B, D))) * t)
    wkv_den = bf(0.5 + 1.5 * np.random.uniform(0.0, 1.0, (B, D)))
    w_o = np.random.standard_normal((E, D)) * 2.0 / np.sqrt(D) / t[None, :]
    wo_words, wo_scales = pack_weight(np.ascontiguousarray(w_o.T), FMT)
    return {
        "x": x,
        "state_x": state_x,
        "time_mix_r": time_mix_r,
        "W_receptance_words": wr_words,
        "W_receptance_scales": wr_scales,
        "wkv_num": wkv_num,
        "wkv_den": wkv_den,
        "W_output_words": wo_words,
        "W_output_scales": wo_scales,
    }


def reference(x, state_x, time_mix_r, W_receptance_words, W_receptance_scales, wkv_num, wkv_den, W_output_words, W_output_scales):
    x, state_x, mr = f64(x), f64(state_x), f64(time_mix_r)
    xr = x * mr + state_x * (1.0 - mr)
    r = hard_sigmoid(mxq(xr, 1, "e4m3") @ unpack_weight(W_receptance_words, W_receptance_scales, FMT))
    h = r * f64(wkv_num) / f64(wkv_den)
    return mxq(h, 1, "e4m3") @ unpack_weight(W_output_words, W_output_scales, FMT)

@@ -1,0 +1,287 @@
+import concourse.mybir as mybir
+from concourse.masks import make_identity
+
+F32 = mybir.dt.float32
+BF16 = mybir.dt.bfloat16
+U8 = mybir.dt.uint8
+U32 = mybir.dt.uint32
+I32 = mybir.dt.int32
+FP8X4 = mybir.dt.float8_e4m3fn_x4
+ALU = mybir.AluOpType
+ACT = mybir.ActivationFunctionType
+
+P = 128
+PACK = 4
+PAIR = 2
+K_PASS = P * PACK
+EMBED = 16384
+HIDDEN = 512
+N_TILE = 512
+PASSES = EMBED // K_PASS
+CHUNK = 4
+CHUNKS = PASSES // CHUNK
+ROUND = 2
+SCALE_ROWS = 16
+SHARED = 4
+PLANE_COLS = PASSES // SHARED
+ROUNDS = PASSES // ROUND
+AHEAD = 2
+PASS_WORDS = K_PASS // PAIR
+
+FLOPS = 2 * 2 * P * EMBED * HIDDEN
+
+
+def scale_plane(planes, number):
+    return planes[PACK * (number // PLANE_COLS) : P, number % PLANE_COLS, :]
+
+
+def tile_rwkv_timemix_for_quant_pb_k_kernel(
+    tc,
+    x,
+    state_x,
+    time_mix_r,
+    w_receptance_words,
+    w_receptance_scales,
+    wkv_num,
+    wkv_den,
+    w_output_words,
+    w_output_scales,
+    out,
+):
+    nc = tc.nc
+    chunk_k = CHUNK * K_PASS
+    chunk_words = CHUNK * N_TILE
+
+    with (
+        tc.manual_schedule(),
+        tc.tile_pool(name="keep", bufs=1) as keep,
+        tc.tile_pool(name="wo", bufs=CHUNKS) as wo_pool,
+    ):
+        identity = keep.tile([P, P], F32)
+        make_identity(nc, identity[:])
+
+        mix_rows = keep.tile([P, PASS_WORDS], F32)
+        nc.vector.memset(mix_rows[:], 0.0)
+
+        wr_planes = keep.tile([P, PLANE_COLS, N_TILE], U8, align_bytes=64)
+        wo_planes = keep.tile([P, PLANE_COLS, N_TILE], U8, align_bytes=64)
+        nc.vector.memset(wr_planes[:].rearrange("p j n -> p (j n)").bitcast(I32), 0)
+        nc.vector.memset(wo_planes[:].rearrange("p j n -> p (j n)").bitcast(I32), 0)
+
+        num = keep.tile([P, HIDDEN], BF16)
+        den = keep.tile([P, HIDDEN], BF16)
+        ratio = keep.tile([P, PACK, P], F32)
+        h_codes = keep.tile([P, P], U32, align_bytes=64)
+        h_scales = keep.tile([P, P], U8, align_bytes=64)
+
+        with (
+            tc.psum_pool(name="acc", bufs=1) as acc_pool,
+            tc.psum_pool(name="turned", bufs=AHEAD + 1) as turned_pool,
+            tc.psum_pool(name="small", bufs=1) as small_pool,
+        ):
+            with (
+                tc.tile_pool(name="x", bufs=CHUNKS) as x_pool,
+                tc.tile_pool(name="wr", bufs=CHUNKS) as wr_pool,
+                tc.tile_pool(name="work", bufs=2) as work,
+            ):
+                nc.sync.dma_start(
+                    out=mix_rows[0:PASSES, :].bitcast(BF16),
+                    in_=time_mix_r.rearrange("o (g k) -> (o g) k", k=K_PASS),
+                )
+                nc.sync.dma_start(out=den[:], in_=wkv_den)
+                nc.sync.dma_start(out=num[:], in_=wkv_num)
+                x_chunks, old_chunks, wr_chunks, wo_chunks = [], [], [], []
+                for c in range(CHUNKS):
+                    k_cols = slice(c * chunk_k, (c + 1) * chunk_k)
+                    x_chunk = x_pool.tile([P, chunk_k], BF16)
+                    nc.sync.dma_start(out=x_chunk[:], in_=x[:, k_cols])
+                    x_chunks.append(x_chunk)
+                    old_chunk = x_pool.tile([P, chunk_k], BF16)
+                    nc.sync.dma_start(out=old_chunk[:], in_=state_x[:, k_cols])
+                    old_chunks.append(old_chunk)
+                    if c == 0:
+                        for q in range(SCALE_ROWS):
+                            top = 32 * (q // 4) + q % 4
+                            nc.sync.dma_start(
+                                out=wr_planes[top : top + PACK * SHARED : PACK, :, :].bitcast(I32),
+                                in_=w_receptance_scales[:, q, :]
+                                .rearrange("(i j) n -> i j n", i=SHARED)
+                                .bitcast(I32),
+                            )
+                    wr_chunk = wr_pool.tile([P, CHUNK, N_TILE], U32, align_bytes=64)
+                    nc.sync.dma_start(
+                        out=wr_chunk[:].bitcast(I32),
+                        in_=w_receptance_words[c * CHUNK : (c + 1) * CHUNK]
+                        .rearrange("g p n t -> p g (n t)")
+                        .bitcast(I32),
+                    )
+                    wr_chunks.append(wr_chunk)
+                for quadrant in range(SCALE_ROWS // PACK):
+                    nc.sync.dma_start(
+                        out=wo_planes[32 * quadrant : 32 * quadrant + PACK * SHARED, :, :]
+                        .rearrange("p j n -> p (j n)")
+                        .bitcast(I32),
+                        in_=w_output_scales[0, PACK * quadrant : PACK * (quadrant + 1), :]
+                        .rearrange("r (i m) -> i r m", i=SHARED)
+                        .bitcast(I32),
+                    )
+                wo_bytes = w_output_words[0].rearrange("p n t -> p (n t)")
+                for c in range(CHUNKS):
+                    wo_chunk = wo_pool.tile([P, chunk_words], U32, align_bytes=64)
+                    nc.sync.dma_start(
+                        out=wo_chunk[:].bitcast(I32),
+                        in_=wo_bytes[:, c * chunk_words * PACK : (c + 1) * chunk_words * PACK].bitcast(I32),
+                    )
+                    wo_chunks.append(wo_chunk)
+
+                mix_turned = small_pool.tile([P, PAIR, P], F32, tag="small")
+                for u in range(PAIR):
+                    nc.tensor.transpose(mix_turned[:, u, :], mix_rows[:, u:PASS_WORDS:PAIR], identity[:])
+                take_new = keep.tile([P, PASSES * PACK], F32)
+                keep_old = keep.tile([P, PASSES * PACK], F32)
+                nc.vector.tensor_copy(
+                    out=take_new[:].rearrange("p (g u e) -> p g u e", u=PAIR, e=PAIR),
+                    in_=mix_turned[:]
+                    .bitcast(BF16)
+                    .rearrange("p u (g e) -> p g u e", e=PAIR)[:, 0:PASSES, :, :],
+                )
+                nc.vector.tensor_scalar(
+                    out=keep_old[:], in0=take_new[:], scalar1=-1.0, scalar2=1.0, op0=ALU.mult, op1=ALU.add
+                )
+
+                inverse = work.tile([P, HIDDEN], F32)
+                nc.vector.reciprocal(out=inverse[:], in_=den[:])
+                nc.vector.tensor_tensor(
+                    out=ratio[:],
+                    in0=num[:].rearrange("b (p t) -> b t p", t=PACK),
+                    in1=inverse[:].rearrange("b (p t) -> b t p", t=PACK),
+                    op=ALU.mult,
+                )
+
+                acc = acc_pool.tile([P, HIDDEN], F32)
+
+                def turn(r):
+                    c, first = divmod(r * ROUND, CHUNK)
+                    x_words = x_chunks[c][:].bitcast(F32)
+                    old_words = old_chunks[c][:].bitcast(F32)
+                    x_turned = turned_pool.tile([P, ROUND, PAIR, P], F32)
+                    old_turned = turned_pool.tile([P, ROUND, PAIR, P], F32)
+                    for s in range(ROUND):
+                        for u in range(PAIR):
+                            cols = slice((first + s) * PASS_WORDS + u, (first + s + 1) * PASS_WORDS, PAIR)
+                            nc.tensor.transpose(x_turned[:, s, u, :], x_words[:, cols], identity[:])
+                            nc.tensor.transpose(old_turned[:, s, u, :], old_words[:, cols], identity[:])
+                    return x_turned, old_turned
+
+                def mix(r, x_turned, old_turned):
+                    x_pairs = x_turned[:].bitcast(BF16).rearrange("p s u (b e) -> p s u b e", e=PAIR)
+                    old_pairs = old_turned[:].bitcast(BF16).rearrange("p s u (b e) -> p s u b e", e=PAIR)
+                    old_part = work.tile([P, ROUND, PACK, P], F32)
+                    mixed = work.tile([P, ROUND, PACK, P], BF16)
+                    for s in range(ROUND):
+                        for t in range(PACK):
+                            u, e = divmod(t, PAIR)
+                            col = (r * ROUND + s) * PACK + t
+                            nc.scalar.activation(
+                                out=old_part[:, s, t, :],
+                                in_=old_pairs[:, s, u, :, e],
+                                func=ACT.Copy,
+                                scale=keep_old[:, col : col + 1],
+                            )
+                            nc.vector.scalar_tensor_tensor(
+                                out=mixed[:, s, t, :],
+                                in0=x_pairs[:, s, u, :, e],
+                                scalar=take_new[:, col : col + 1],
+                                in1=old_part[:, s, t, :],
+                                op0=ALU.mult,
+                                op1=ALU.add,
+                            )
+                    return mixed
+
+                def regroup(mixed):
+                    grouped = work.tile([P, ROUND, P, PACK], BF16, align_bytes=64)
+                    nc.vector.tensor_copy(out=grouped[:], in_=mixed[:].rearrange("p s t b -> p s b t"))
+                    return grouped
+
+                def quantise_and_multiply(r, grouped):
+                    xr_codes = work.tile([P, ROUND * P], U32, align_bytes=64)
+                    xr_scales = work.tile([P, ROUND * P], U8, align_bytes=64)
+                    nc.vector.quantize_mx(
+                        out=xr_codes[:].bitcast(FP8X4),
+                        scales=xr_scales[:],
+                        in_=grouped[:].rearrange("p s b t -> p (s b t)"),
+                    )
+                    for s in range(ROUND):
+                        g = r * ROUND + s
+                        rows = slice(s * P, (s + 1) * P)
+                        nc.tensor.matmul_mx(
+                            out=acc[:],
+                            lhsT=xr_codes[:, rows].bitcast(FP8X4),
+                            lhsT_scale=xr_scales[:, rows],
+                            rhs=wr_chunks[g // CHUNK][:, g % CHUNK, :].bitcast(FP8X4),
+                            rhs_scale=scale_plane(wr_planes, g),
+                            start=(g == 0),
+                            stop=(g == PASSES - 1),
+                        )
+
+                turned = [turn(r) for r in range(AHEAD)]
+                grouped = None
+                for r in range(ROUNDS):
+                    if r + AHEAD < ROUNDS:
+                        turned.append(turn(r + AHEAD))
+                    mixed = mix(r, turned[r][0], turned[r][1])
+                    if r > 0:
+                        quantise_and_multiply(r - 1, grouped)
+                    grouped = regroup(mixed)
+                quantise_and_multiply(ROUNDS - 1, grouped)
+
+            with tc.tile_pool(name="gate", bufs=1) as gate_pool:
+                lifted = gate_pool.tile([P, PACK, P], F32)
+                nc.scalar.activation(
+                    out=lifted[:],
+                    in_=acc[:].rearrange("b (p t) -> b t p", t=PACK),
+                    func=ACT.Relu,
+                    scale=1.0 / 6.0,
+                    bias=0.5,
+                )
+                h = gate_pool.tile([P, PACK, P], F32)
+                nc.vector.scalar_tensor_tensor(
+                    out=h[:], in0=lifted[:], scalar=1.0, in1=ratio[:], op0=ALU.min, op1=ALU.mult
+                )
+                h_turned = small_pool.tile([P, PACK, P], F32, tag="small")
+                for t in range(PACK):
+                    nc.tensor.transpose(h_turned[:, t, :], h[:, t, :], identity[:])
+                h_grouped = gate_pool.tile([P, P, PACK], BF16, align_bytes=64)
+                nc.vector.tensor_copy(out=h_grouped[:], in_=h_turned[:].rearrange("p t b -> p b t"))
+                nc.vector.quantize_mx(
+                    out=h_codes[:].bitcast(FP8X4),
+                    scales=h_scales[:],
+                    in_=h_grouped[:].rearrange("p b t -> p (b t)"),
+                )
+
+        with (
+            tc.psum_pool(name="bank", bufs=8) as bank_pool,
+            tc.tile_pool(name="result", bufs=CHUNKS) as result_pool,
+        ):
+            for c in range(CHUNKS):
+                result = result_pool.tile([P, CHUNK, N_TILE], F32)
+                for v in range(CHUNK):
+                    j = c * CHUNK + v
+                    bank = bank_pool.tile([P, N_TILE], F32)
+                    nc.tensor.matmul_mx(
+                        out=bank[:],
+                        lhsT=h_codes[:].bitcast(FP8X4),
+                        lhsT_scale=h_scales[:],
+                        rhs=wo_chunks[c][:, v * N_TILE : (v + 1) * N_TILE].bitcast(FP8X4),
+                        rhs_scale=scale_plane(wo_planes, j),
+                        start=True,
+                        stop=True,
+                    )
+                    if j % 2 == 0:
+                        nc.scalar.copy(out=result[:, v, :], in_=bank[:])
+                    else:
+                        nc.vector.tensor_copy(out=result[:, v, :], in_=bank[:])
+                nc.sync.dma_start(
+                    out=out[:, c * CHUNK * N_TILE : (c + 1) * CHUNK * N_TILE],
+                    in_=result[:].rearrange("p v n -> p (v n)"),
+                )

@@ -18,21 +18,26 @@ EMBED = 16384
 HIDDEN = 512
 N_TILE = 512
 PASSES = EMBED // K_PASS
+OUT_TILES = EMBED // N_TILE
 CHUNK = 4
 CHUNKS = PASSES // CHUNK
+OUT_CHUNK = 8
+OUT_CHUNKS = OUT_TILES // OUT_CHUNK
 ROUND = 2
 SCALE_ROWS = 16
 SHARED = 4
-PLANE_COLS = PASSES // SHARED
+BLOCKS = PASSES // SHARED
 ROUNDS = PASSES // ROUND
 AHEAD = 2
 PASS_WORDS = K_PASS // PAIR
 
+assert CHUNK == SHARED
+
 FLOPS = 2 * 2 * P * EMBED * HIDDEN
 
 
-def scale_plane(planes, number):
-    return planes[PACK * (number // PLANE_COLS) : P, number % PLANE_COLS, :]
+def scale_plane(planes, i, block):
+    return planes[PACK * i : P, block, :]
 
 
 def tile_rwkv_timemix_for_quant_pb_k_kernel(
@@ -50,12 +55,12 @@ def tile_rwkv_timemix_for_quant_pb_k_kernel(
 ):
     nc = tc.nc
     chunk_k = CHUNK * K_PASS
-    chunk_words = CHUNK * N_TILE
+    out_cols = OUT_CHUNK * N_TILE
 
     with (
         tc.manual_schedule(),
         tc.tile_pool(name="keep", bufs=1) as keep,
-        tc.tile_pool(name="wo", bufs=CHUNKS) as wo_pool,
+        tc.tile_pool(name="wo", bufs=OUT_CHUNKS) as wo_pool,
     ):
         identity = keep.tile([P, P], F32)
         make_identity(nc, identity[:])
@@ -63,8 +68,8 @@ def tile_rwkv_timemix_for_quant_pb_k_kernel(
         mix_rows = keep.tile([P, PASS_WORDS], F32)
         nc.vector.memset(mix_rows[:], 0.0)
 
-        wr_planes = keep.tile([P, PLANE_COLS, N_TILE], U8, align_bytes=64)
-        wo_planes = keep.tile([P, PLANE_COLS, N_TILE], U8, align_bytes=64)
+        wr_planes = keep.tile([P, BLOCKS, N_TILE], U8, align_bytes=64)
+        wo_planes = keep.tile([P, BLOCKS, N_TILE], U8, align_bytes=64)
         nc.vector.memset(wr_planes[:].rearrange("p j n -> p (j n)").bitcast(I32), 0)
         nc.vector.memset(wo_planes[:].rearrange("p j n -> p (j n)").bitcast(I32), 0)
 
@@ -84,10 +89,6 @@ def tile_rwkv_timemix_for_quant_pb_k_kernel(
                 tc.tile_pool(name="wr", bufs=CHUNKS) as wr_pool,
                 tc.tile_pool(name="work", bufs=2) as work,
             ):
-                nc.sync.dma_start(
-                    out=mix_rows[0:PASSES, :].bitcast(BF16),
-                    in_=time_mix_r.rearrange("o (g k) -> (o g) k", k=K_PASS),
-                )
                 nc.sync.dma_start(out=den[:], in_=wkv_den)
                 nc.sync.dma_start(out=num[:], in_=wkv_num)
                 x_chunks, old_chunks, wr_chunks, wo_chunks = [], [], [], []
@@ -100,20 +101,22 @@ def tile_rwkv_timemix_for_quant_pb_k_kernel(
                     nc.sync.dma_start(out=old_chunk[:], in_=state_x[:, k_cols])
                     old_chunks.append(old_chunk)
                     if c == 0:
-                        for q in range(SCALE_ROWS):
-                            top = 32 * (q // 4) + q % 4
-                            nc.sync.dma_start(
-                                out=wr_planes[top : top + PACK * SHARED : PACK, :, :].bitcast(I32),
-                                in_=w_receptance_scales[:, q, :]
-                                .rearrange("(i j) n -> i j n", i=SHARED)
-                                .bitcast(I32),
-                            )
+                        nc.sync.dma_start(
+                            out=mix_rows[0:PASSES, :].bitcast(BF16),
+                            in_=time_mix_r.rearrange("o (g k) -> (o g) k", k=K_PASS),
+                        )
+                    passes = slice(c * CHUNK, (c + 1) * CHUNK)
+                    for quadrant in range(SCALE_ROWS // PACK):
+                        nc.sync.dma_start(
+                            out=wr_planes[32 * quadrant : 32 * quadrant + PACK * SHARED, c, :].bitcast(I32),
+                            in_=w_receptance_scales[
+                                passes, PACK * quadrant : PACK * (quadrant + 1), :
+                            ].bitcast(I32),
+                        )
                     wr_chunk = wr_pool.tile([P, CHUNK, N_TILE], U32, align_bytes=64)
                     nc.sync.dma_start(
                         out=wr_chunk[:].bitcast(I32),
-                        in_=w_receptance_words[c * CHUNK : (c + 1) * CHUNK]
-                        .rearrange("g p n t -> p g (n t)")
-                        .bitcast(I32),
+                        in_=w_receptance_words[passes].rearrange("g p n t -> p g (n t)").bitcast(I32),
                     )
                     wr_chunks.append(wr_chunk)
                 for quadrant in range(SCALE_ROWS // PACK):
@@ -126,13 +129,22 @@ def tile_rwkv_timemix_for_quant_pb_k_kernel(
                         .bitcast(I32),
                     )
                 wo_bytes = w_output_words[0].rearrange("p n t -> p (n t)")
-                for c in range(CHUNKS):
-                    wo_chunk = wo_pool.tile([P, chunk_words], U32, align_bytes=64)
+                for c in range(OUT_CHUNKS):
+                    wo_chunk = wo_pool.tile([P, out_cols], U32, align_bytes=64)
                     nc.sync.dma_start(
                         out=wo_chunk[:].bitcast(I32),
-                        in_=wo_bytes[:, c * chunk_words * PACK : (c + 1) * chunk_words * PACK].bitcast(I32),
+                        in_=wo_bytes[:, c * out_cols * PACK : (c + 1) * out_cols * PACK].bitcast(I32),
                     )
                     wo_chunks.append(wo_chunk)
+
+                inverse = work.tile([P, HIDDEN], F32)
+                nc.vector.reciprocal(out=inverse[:], in_=den[:])
+                nc.vector.tensor_tensor(
+                    out=ratio[:],
+                    in0=num[:].rearrange("b (p t) -> b t p", t=PACK),
+                    in1=inverse[:].rearrange("b (p t) -> b t p", t=PACK),
+                    op=ALU.mult,
+                )
 
                 mix_turned = small_pool.tile([P, PAIR, P], F32, tag="small")
                 for u in range(PAIR):
@@ -147,15 +159,6 @@ def tile_rwkv_timemix_for_quant_pb_k_kernel(
                 )
                 nc.vector.tensor_scalar(
                     out=keep_old[:], in0=take_new[:], scalar1=-1.0, scalar2=1.0, op0=ALU.mult, op1=ALU.add
-                )
-
-                inverse = work.tile([P, HIDDEN], F32)
-                nc.vector.reciprocal(out=inverse[:], in_=den[:])
-                nc.vector.tensor_tensor(
-                    out=ratio[:],
-                    in0=num[:].rearrange("b (p t) -> b t p", t=PACK),
-                    in1=inverse[:].rearrange("b (p t) -> b t p", t=PACK),
-                    op=ALU.mult,
                 )
 
                 acc = acc_pool.tile([P, HIDDEN], F32)
@@ -219,7 +222,7 @@ def tile_rwkv_timemix_for_quant_pb_k_kernel(
                             lhsT=xr_codes[:, rows].bitcast(FP8X4),
                             lhsT_scale=xr_scales[:, rows],
                             rhs=wr_chunks[g // CHUNK][:, g % CHUNK, :].bitcast(FP8X4),
-                            rhs_scale=scale_plane(wr_planes, g),
+                            rhs_scale=scale_plane(wr_planes, g % CHUNK, g // CHUNK),
                             start=(g == 0),
                             stop=(g == PASSES - 1),
                         )
@@ -261,19 +264,19 @@ def tile_rwkv_timemix_for_quant_pb_k_kernel(
 
         with (
             tc.psum_pool(name="bank", bufs=8) as bank_pool,
-            tc.tile_pool(name="result", bufs=CHUNKS) as result_pool,
+            tc.tile_pool(name="result", bufs=OUT_CHUNKS) as result_pool,
         ):
-            for c in range(CHUNKS):
-                result = result_pool.tile([P, CHUNK, N_TILE], F32)
-                for v in range(CHUNK):
-                    j = c * CHUNK + v
+            for c in range(OUT_CHUNKS):
+                result = result_pool.tile([P, OUT_CHUNK, N_TILE], F32)
+                for v in range(OUT_CHUNK):
+                    j = c * OUT_CHUNK + v
                     bank = bank_pool.tile([P, N_TILE], F32)
                     nc.tensor.matmul_mx(
                         out=bank[:],
                         lhsT=h_codes[:].bitcast(FP8X4),
                         lhsT_scale=h_scales[:],
                         rhs=wo_chunks[c][:, v * N_TILE : (v + 1) * N_TILE].bitcast(FP8X4),
-                        rhs_scale=scale_plane(wo_planes, j),
+                        rhs_scale=scale_plane(wo_planes, j // BLOCKS, j % BLOCKS),
                         start=True,
                         stop=True,
                     )
@@ -282,6 +285,6 @@ def tile_rwkv_timemix_for_quant_pb_k_kernel(
                     else:
                         nc.vector.tensor_copy(out=result[:, v, :], in_=bank[:])
                 nc.sync.dma_start(
-                    out=out[:, c * CHUNK * N_TILE : (c + 1) * CHUNK * N_TILE],
+                    out=out[:, c * out_cols : (c + 1) * out_cols],
                     in_=result[:].rearrange("p v n -> p (v n)"),
                 )

@@ -21,6 +21,8 @@ PASSES = EMBED // K_PASS
 OUT_TILES = EMBED // N_TILE
 CHUNK = 4
 CHUNKS = PASSES // CHUNK
+X_CHUNK = 8
+X_CHUNKS = PASSES // X_CHUNK
 OUT_CHUNK = 8
 OUT_CHUNKS = OUT_TILES // OUT_CHUNK
 ROUND = 2
@@ -54,7 +56,7 @@ def tile_rwkv_timemix_for_quant_pb_k_kernel(
     out,
 ):
     nc = tc.nc
-    chunk_k = CHUNK * K_PASS
+    chunk_k = X_CHUNK * K_PASS
     out_cols = OUT_CHUNK * N_TILE
 
     with (
@@ -85,7 +87,7 @@ def tile_rwkv_timemix_for_quant_pb_k_kernel(
             tc.psum_pool(name="small", bufs=1) as small_pool,
         ):
             with (
-                tc.tile_pool(name="x", bufs=CHUNKS) as x_pool,
+                tc.tile_pool(name="x", bufs=X_CHUNKS) as x_pool,
                 tc.tile_pool(name="wr", bufs=CHUNKS) as wr_pool,
                 tc.tile_pool(name="work", bufs=2) as work,
             ):
@@ -93,13 +95,14 @@ def tile_rwkv_timemix_for_quant_pb_k_kernel(
                 nc.sync.dma_start(out=num[:], in_=wkv_num)
                 x_chunks, old_chunks, wr_chunks, wo_chunks = [], [], [], []
                 for c in range(CHUNKS):
-                    k_cols = slice(c * chunk_k, (c + 1) * chunk_k)
-                    x_chunk = x_pool.tile([P, chunk_k], BF16)
-                    nc.sync.dma_start(out=x_chunk[:], in_=x[:, k_cols])
-                    x_chunks.append(x_chunk)
-                    old_chunk = x_pool.tile([P, chunk_k], BF16)
-                    nc.sync.dma_start(out=old_chunk[:], in_=state_x[:, k_cols])
-                    old_chunks.append(old_chunk)
+                    if c % (X_CHUNK // CHUNK) == 0:
+                        first_k = c * CHUNK * K_PASS
+                        x_chunk = x_pool.tile([P, chunk_k], BF16)
+                        nc.sync.dma_start(out=x_chunk[:], in_=x[:, first_k : first_k + chunk_k])
+                        x_chunks.append(x_chunk)
+                        old_chunk = x_pool.tile([P, chunk_k], BF16)
+                        nc.sync.dma_start(out=old_chunk[:], in_=state_x[:, first_k : first_k + chunk_k])
+                        old_chunks.append(old_chunk)
                     if c == 0:
                         nc.sync.dma_start(
                             out=mix_rows[0:PASSES, :].bitcast(BF16),
@@ -164,7 +167,7 @@ def tile_rwkv_timemix_for_quant_pb_k_kernel(
                 acc = acc_pool.tile([P, HIDDEN], F32)
 
                 def turn(r):
-                    c, first = divmod(r * ROUND, CHUNK)
+                    c, first = divmod(r * ROUND, X_CHUNK)
                     x_words = x_chunks[c][:].bitcast(F32)
                     old_words = old_chunks[c][:].bitcast(F32)
                     x_turned = turned_pool.tile([P, ROUND, PAIR, P], F32)

@@ -30,6 +30,7 @@ SCALE_ROWS = 16
 SHARED = 4
 BLOCKS = PASSES // SHARED
 ROUNDS = PASSES // ROUND
+SCALES_BEHIND = 2
 AHEAD = 2
 PASS_WORDS = K_PASS // PAIR
 
@@ -94,34 +95,44 @@ def tile_rwkv_timemix_for_quant_pb_k_kernel(
                 nc.sync.dma_start(out=den[:], in_=wkv_den)
                 nc.sync.dma_start(out=num[:], in_=wkv_num)
                 x_chunks, old_chunks, wr_chunks, wo_chunks = [], [], [], []
+
+                scale_loads = [(c, quadrant) for c in range(CHUNKS) for quadrant in range(SCALE_ROWS // PACK)]
+
+                def load_scales(count):
+                    for c, quadrant in scale_loads[:count]:
+                        nc.sync.dma_start(
+                            out=wr_planes[32 * quadrant : 32 * quadrant + PACK * SHARED, c, :].bitcast(I32),
+                            in_=w_receptance_scales[
+                                c * CHUNK : (c + 1) * CHUNK, PACK * quadrant : PACK * (quadrant + 1), :
+                            ].bitcast(I32),
+                        )
+                    scale_loads[:count] = []
+
                 for c in range(CHUNKS):
                     if c % (X_CHUNK // CHUNK) == 0:
                         first_k = c * CHUNK * K_PASS
                         x_chunk = x_pool.tile([P, chunk_k], BF16)
                         nc.sync.dma_start(out=x_chunk[:], in_=x[:, first_k : first_k + chunk_k])
                         x_chunks.append(x_chunk)
+                        load_scales(SCALES_BEHIND)
                         old_chunk = x_pool.tile([P, chunk_k], BF16)
                         nc.sync.dma_start(out=old_chunk[:], in_=state_x[:, first_k : first_k + chunk_k])
                         old_chunks.append(old_chunk)
-                    if c == 0:
-                        nc.sync.dma_start(
-                            out=mix_rows[0:PASSES, :].bitcast(BF16),
-                            in_=time_mix_r.rearrange("o (g k) -> (o g) k", k=K_PASS),
-                        )
-                    passes = slice(c * CHUNK, (c + 1) * CHUNK)
-                    for quadrant in range(SCALE_ROWS // PACK):
-                        nc.sync.dma_start(
-                            out=wr_planes[32 * quadrant : 32 * quadrant + PACK * SHARED, c, :].bitcast(I32),
-                            in_=w_receptance_scales[
-                                passes, PACK * quadrant : PACK * (quadrant + 1), :
-                            ].bitcast(I32),
-                        )
+                        if c == 0:
+                            nc.sync.dma_start(
+                                out=mix_rows[0:PASSES, :].bitcast(BF16),
+                                in_=time_mix_r.rearrange("o (g k) -> (o g) k", k=K_PASS),
+                            )
+                        load_scales(SCALES_BEHIND)
                     wr_chunk = wr_pool.tile([P, CHUNK, N_TILE], U32, align_bytes=64)
                     nc.sync.dma_start(
                         out=wr_chunk[:].bitcast(I32),
-                        in_=w_receptance_words[passes].rearrange("g p n t -> p g (n t)").bitcast(I32),
+                        in_=w_receptance_words[c * CHUNK : (c + 1) * CHUNK]
+                        .rearrange("g p n t -> p g (n t)")
+                        .bitcast(I32),
                     )
                     wr_chunks.append(wr_chunk)
+                    load_scales(SCALES_BEHIND)
                 for quadrant in range(SCALE_ROWS // PACK):
                     nc.sync.dma_start(
                         out=wo_planes[32 * quadrant : 32 * quadrant + PACK * SHARED, :, :]

@@ -71,6 +71,10 @@ def tile_rwkv_timemix_for_quant_pb_k_kernel(
         mix_rows = keep.tile([P, PASS_WORDS], F32)
         nc.vector.memset(mix_rows[:], 0.0)
 
+        first_column = keep.tile([P, 2], F32)
+        nc.vector.memset(first_column[:], 0.0)
+        nc.scalar.activation(out=first_column[:, 1:2], in_=first_column[:, 0:1], func=ACT.Copy, scale=1.0)
+
         wr_planes = keep.tile([P, BLOCKS, N_TILE], U8, align_bytes=64)
         wo_planes = keep.tile([P, BLOCKS, N_TILE], U8, align_bytes=64)
         nc.vector.memset(wr_planes[:].rearrange("p j n -> p (j n)").bitcast(I32), 0)
@@ -217,7 +221,14 @@ def tile_rwkv_timemix_for_quant_pb_k_kernel(
 
                 def regroup(mixed):
                     grouped = work.tile([P, ROUND, P, PACK], BF16, align_bytes=64)
-                    nc.vector.tensor_copy(out=grouped[:], in_=mixed[:].rearrange("p s t b -> p s b t"))
+                    nc.gpsimd.tensor_scalar(
+                        out=grouped[:],
+                        in0=mixed[:].rearrange("p s t b -> p s b t"),
+                        scalar1=1.0,
+                        scalar2=0.0,
+                        op0=ALU.mult,
+                        op1=ALU.add,
+                    )
                     return grouped
 
                 def quantise_and_multiply(r, grouped):

@@ -30,7 +30,10 @@ SCALE_ROWS = 16
 SHARED = 4
 BLOCKS = PASSES // SHARED
 ROUNDS = PASSES // ROUND
-SCALES_BEHIND = 2
+QUADRANTS = SCALE_ROWS // PACK
+MOVED = PACK * SHARED
+SPAN = 2
+MOVES_BEHIND = 3
 AHEAD = 2
 PASS_WORDS = K_PASS // PAIR
 
@@ -100,17 +103,52 @@ def tile_rwkv_timemix_for_quant_pb_k_kernel(
                 nc.sync.dma_start(out=num[:], in_=wkv_num)
                 x_chunks, old_chunks, wr_chunks, wo_chunks = [], [], [], []
 
-                scale_loads = [(c, quadrant) for c in range(CHUNKS) for quadrant in range(SCALE_ROWS // PACK)]
+                wr_staged = keep.tile([P, QUADRANTS, N_TILE], U8, align_bytes=64)
+                for quadrant in range(QUADRANTS):
+                    nc.sync.dma_start(
+                        out=wr_staged[:, quadrant, :].bitcast(I32),
+                        in_=w_receptance_scales[:, PACK * quadrant : PACK * (quadrant + 1), :].bitcast(I32),
+                    )
 
-                def load_scales(count):
-                    for c, quadrant in scale_loads[:count]:
+                wo_staged = keep.tile([P, QUADRANTS // 2, SPAN * N_TILE], U8, align_bytes=64)
+
+                def stage_output_scales():
+                    for quadrant in range(QUADRANTS):
+                        half = P // 2 * (quadrant % 2)
                         nc.sync.dma_start(
-                            out=wr_planes[32 * quadrant : 32 * quadrant + PACK * SHARED, c, :].bitcast(I32),
-                            in_=w_receptance_scales[
-                                c * CHUNK : (c + 1) * CHUNK, PACK * quadrant : PACK * (quadrant + 1), :
-                            ].bitcast(I32),
+                            out=wo_staged[half : half + P // 2, quadrant // 2, :].bitcast(I32),
+                            in_=w_output_scales[0, PACK * quadrant : PACK * (quadrant + 1), :]
+                            .rearrange("r (s m) -> s r m", m=SPAN * N_TILE)
+                            .bitcast(I32),
                         )
-                    scale_loads[:count] = []
+
+                moves = []
+                for c in range(CHUNKS):
+                    for quadrant in range(QUADRANTS):
+                        first = 32 * quadrant
+                        moves.append(
+                            (
+                                wr_planes[first : first + MOVED, c, :],
+                                wr_staged[MOVED * c : MOVED * (c + 1), quadrant, :],
+                            )
+                        )
+                for y in range(BLOCKS // SPAN):
+                    for quadrant in range(QUADRANTS):
+                        first = 32 * quadrant
+                        source = P // 2 * (quadrant % 2) + MOVED * y
+                        moves.append(
+                            (
+                                wo_planes[first : first + MOVED, SPAN * y : SPAN * (y + 1), :].rearrange(
+                                    "p j n -> p (j n)"
+                                ),
+                                wo_staged[source : source + MOVED, quadrant // 2, :],
+                            )
+                        )
+
+                def move_scales():
+                    for target, source in moves[:MOVES_BEHIND]:
+                        nc.sync.dma_start(out=target.bitcast(I32), in_=source.bitcast(I32))
+                    moves[:MOVES_BEHIND] = []
 
                 for c in range(CHUNKS):
                     if c % (X_CHUNK // CHUNK) == 0:
@@ -118,16 +156,19 @@ def tile_rwkv_timemix_for_quant_pb_k_kernel(
                         x_chunk = x_pool.tile([P, chunk_k], BF16)
                         nc.sync.dma_start(out=x_chunk[:], in_=x[:, first_k : first_k + chunk_k])
                         x_chunks.append(x_chunk)
-                        load_scales(SCALES_BEHIND)
-                        old_chunk = x_pool.tile([P, chunk_k], BF16)
-                        nc.sync.dma_start(out=old_chunk[:], in_=state_x[:, first_k : first_k + chunk_k])
-                        old_chunks.append(old_chunk)
                         if c == 0:
                             nc.sync.dma_start(
                                 out=mix_rows[0:PASSES, :].bitcast(BF16),
                                 in_=time_mix_r.rearrange("o (g k) -> (o g) k", k=K_PASS),
                             )
-                        load_scales(SCALES_BEHIND)
+                        else:
+                            move_scales()
+                        old_chunk = x_pool.tile([P, chunk_k], BF16)
+                        nc.sync.dma_start(out=old_chunk[:], in_=state_x[:, first_k : first_k + chunk_k])
+                        old_chunks.append(old_chunk)
+                        move_scales()
+                        if c == 0:
+                            move_scales()
                     wr_chunk = wr_pool.tile([P, CHUNK, N_TILE], U32, align_bytes=64)
                     nc.sync.dma_start(
                         out=wr_chunk[:].bitcast(I32),
@@ -136,16 +177,9 @@ def tile_rwkv_timemix_for_quant_pb_k_kernel(
                         .bitcast(I32),
                     )
                     wr_chunks.append(wr_chunk)
-                    load_scales(SCALES_BEHIND)
-                for quadrant in range(SCALE_ROWS // PACK):
-                    nc.sync.dma_start(
-                        out=wo_planes[32 * quadrant : 32 * quadrant + PACK * SHARED, :, :]
-                        .rearrange("p j n -> p (j n)")
-                        .bitcast(I32),
-                        in_=w_output_scales[0, PACK * quadrant : PACK * (quadrant + 1), :]
-                        .rearrange("r (i m) -> i r m", i=SHARED)
-                        .bitcast(I32),
-                    )
+                    if c == CHUNKS // 2 - 1:
+                        stage_output_scales()
+                    move_scales()
                 wo_bytes = w_output_words[0].rearrange("p n t -> p (n t)")
                 for c in range(OUT_CHUNKS):
                     wo_chunk = wo_pool.tile([P, out_cols], U32, align_bytes=64)
@@ -301,7 +335,11 @@ def tile_rwkv_timemix_for_quant_pb_k_kernel(
                         lhsT=h_codes[:].bitcast(FP8X4),
                         lhsT_scale=h_scales[:],
                         rhs=wo_chunks[c][:, v * N_TILE : (v + 1) * N_TILE].bitcast(FP8X4),
-                        rhs_scale=scale_plane(wo_planes, j // BLOCKS, j % BLOCKS),
+                        rhs_scale=scale_plane(
+                            wo_planes,
+                            j // SPAN % SHARED,
+                            j // (SPAN * SHARED) * SPAN + j % SPAN,
+                        ),
                         start=True,
                         stop=True,
                     )

@@ -33,7 +33,7 @@ ROUNDS = PASSES // ROUND
 QUADRANTS = SCALE_ROWS // PACK
 MOVED = PACK * SHARED
 SPAN = 2
-MOVES_BEHIND = 3
+MOVES_BEHIND = 2
 AHEAD = 2
 PASS_WORDS = K_PASS // PAIR
 
@@ -112,15 +112,14 @@ def tile_rwkv_timemix_for_quant_pb_k_kernel(
 
                 wo_staged = keep.tile([P, QUADRANTS // 2, SPAN * N_TILE], U8, align_bytes=64)
 
-                def stage_output_scales():
-                    for quadrant in range(QUADRANTS):
-                        half = P // 2 * (quadrant % 2)
-                        nc.sync.dma_start(
-                            out=wo_staged[half : half + P // 2, quadrant // 2, :].bitcast(I32),
-                            in_=w_output_scales[0, PACK * quadrant : PACK * (quadrant + 1), :]
-                            .rearrange("r (s m) -> s r m", m=SPAN * N_TILE)
-                            .bitcast(I32),
-                        )
+                def stage_output_scales(quadrant):
+                    half = P // 2 * (quadrant % 2)
+                    nc.sync.dma_start(
+                        out=wo_staged[half : half + P // 2, quadrant // 2, :].bitcast(I32),
+                        in_=w_output_scales[0, PACK * quadrant : PACK * (quadrant + 1), :]
+                        .rearrange("r (s m) -> s r m", m=SPAN * N_TILE)
+                        .bitcast(I32),
+                    )
 
                 moves = []
                 for c in range(CHUNKS):
@@ -145,10 +144,10 @@ def tile_rwkv_timemix_for_quant_pb_k_kernel(
                             )
                         )
 
-                def move_scales():
-                    for target, source in moves[:MOVES_BEHIND]:
+                def move_scales(count):
+                    for target, source in moves[:count]:
                         nc.sync.dma_start(out=target.bitcast(I32), in_=source.bitcast(I32))
-                    moves[:MOVES_BEHIND] = []
+                    moves[:count] = []
 
                 for c in range(CHUNKS):
                     if c % (X_CHUNK // CHUNK) == 0:
@@ -162,13 +161,11 @@ def tile_rwkv_timemix_for_quant_pb_k_kernel(
                                 in_=time_mix_r.rearrange("o (g k) -> (o g) k", k=K_PASS),
                             )
                         else:
-                            move_scales()
+                            move_scales(MOVES_BEHIND)
                         old_chunk = x_pool.tile([P, chunk_k], BF16)
                         nc.sync.dma_start(out=old_chunk[:], in_=state_x[:, first_k : first_k + chunk_k])
                         old_chunks.append(old_chunk)
-                        move_scales()
-                        if c == 0:
-                            move_scales()
+                        move_scales(MOVES_BEHIND)
                     wr_chunk = wr_pool.tile([P, CHUNK, N_TILE], U32, align_bytes=64)
                     nc.sync.dma_start(
                         out=wr_chunk[:].bitcast(I32),
@@ -177,9 +174,9 @@ def tile_rwkv_timemix_for_quant_pb_k_kernel(
                         .bitcast(I32),
                     )
                     wr_chunks.append(wr_chunk)
-                    if c == CHUNKS // 2 - 1:
-                        stage_output_scales()
-                    move_scales()
+                    move_scales(MOVES_BEHIND)
+                    if c < QUADRANTS:
+                        stage_output_scales(c)
                 wo_bytes = w_output_words[0].rearrange("p n t -> p (n t)")
                 for c in range(OUT_CHUNKS):
                     wo_chunk = wo_pool.tile([P, out_cols], U32, align_bytes=64)
@@ -188,6 +185,7 @@ def tile_rwkv_timemix_for_quant_pb_k_kernel(
                         in_=wo_bytes[:, c * out_cols * PACK : (c + 1) * out_cols * PACK].bitcast(I32),
                     )
                     wo_chunks.append(wo_chunk)
+                    move_scales(QUADRANTS + len(moves) % QUADRANTS)
 
                 inverse = work.tile([P, HIDDEN], F32)
                 nc.vector.reciprocal(out=inverse[:], in_=den[:])

@@ -21,10 +21,11 @@ PASSES = EMBED // K_PASS
 OUT_TILES = EMBED // N_TILE
 CHUNK = 4
 CHUNKS = PASSES // CHUNK
-X_CHUNK = 8
-X_CHUNKS = PASSES // X_CHUNK
+X_PASSES = (4, 8, 8, 12)
+X_FIRST = (0, 4, 12, 20)
 OUT_CHUNK = 8
 OUT_CHUNKS = OUT_TILES // OUT_CHUNK
+STORE_TILES = (4, 4, 8, 8, 8)
 ROUND = 2
 SCALE_ROWS = 16
 SHARED = 4
@@ -33,7 +34,9 @@ ROUNDS = PASSES // ROUND
 QUADRANTS = SCALE_ROWS // PACK
 MOVED = PACK * SHARED
 SPAN = 2
-MOVES_BEHIND = 2
+MOVE_ORDER = (0, 2, 1, 3)
+MOVES_BEHIND_X = 3
+MOVES_BEHIND_W = 2
 AHEAD = 2
 PASS_WORDS = K_PASS // PAIR
 
@@ -60,7 +63,6 @@ def tile_rwkv_timemix_for_quant_pb_k_kernel(
     out,
 ):
     nc = tc.nc
-    chunk_k = X_CHUNK * K_PASS
     out_cols = OUT_CHUNK * N_TILE
 
     with (
@@ -95,7 +97,7 @@ def tile_rwkv_timemix_for_quant_pb_k_kernel(
             tc.psum_pool(name="small", bufs=1) as small_pool,
         ):
             with (
-                tc.tile_pool(name="x", bufs=X_CHUNKS) as x_pool,
+                tc.tile_pool(name="x", bufs=1) as x_pool,
                 tc.tile_pool(name="wr", bufs=CHUNKS) as wr_pool,
                 tc.tile_pool(name="work", bufs=2) as work,
             ):
@@ -104,11 +106,15 @@ def tile_rwkv_timemix_for_quant_pb_k_kernel(
                 x_chunks, old_chunks, wr_chunks, wo_chunks = [], [], [], []
 
                 wr_staged = keep.tile([P, QUADRANTS, N_TILE], U8, align_bytes=64)
-                for quadrant in range(QUADRANTS):
-                    nc.sync.dma_start(
-                        out=wr_staged[:, quadrant, :].bitcast(I32),
-                        in_=w_receptance_scales[:, PACK * quadrant : PACK * (quadrant + 1), :].bitcast(I32),
-                    )
+
+                def stage_receptance_scales():
+                    for quadrant in range(QUADRANTS):
+                        nc.sync.dma_start(
+                            out=wr_staged[:, quadrant, :].bitcast(I32),
+                            in_=w_receptance_scales[
+                                :, PACK * quadrant : PACK * (quadrant + 1), :
+                            ].bitcast(I32),
+                        )
 
                 wo_staged = keep.tile([P, QUADRANTS // 2, SPAN * N_TILE], U8, align_bytes=64)
 
@@ -123,7 +129,7 @@ def tile_rwkv_timemix_for_quant_pb_k_kernel(
 
                 moves = []
                 for c in range(CHUNKS):
-                    for quadrant in range(QUADRANTS):
+                    for quadrant in MOVE_ORDER:
                         first = 32 * quadrant
                         moves.append(
                             (
@@ -132,7 +138,7 @@ def tile_rwkv_timemix_for_quant_pb_k_kernel(
                             )
                         )
                 for y in range(BLOCKS // SPAN):
-                    for quadrant in range(QUADRANTS):
+                    for quadrant in MOVE_ORDER:
                         first = 32 * quadrant
                         source = P // 2 * (quadrant % 2) + MOVED * y
                         moves.append(
@@ -149,34 +155,41 @@ def tile_rwkv_timemix_for_quant_pb_k_kernel(
                         nc.sync.dma_start(out=target.bitcast(I32), in_=source.bitcast(I32))
                     moves[:count] = []
 
-                for c in range(CHUNKS):
-                    if c % (X_CHUNK // CHUNK) == 0:
-                        first_k = c * CHUNK * K_PASS
-                        x_chunk = x_pool.tile([P, chunk_k], BF16)
-                        nc.sync.dma_start(out=x_chunk[:], in_=x[:, first_k : first_k + chunk_k])
-                        x_chunks.append(x_chunk)
-                        if c == 0:
-                            nc.sync.dma_start(
-                                out=mix_rows[0:PASSES, :].bitcast(BF16),
-                                in_=time_mix_r.rearrange("o (g k) -> (o g) k", k=K_PASS),
-                            )
-                        else:
-                            move_scales(MOVES_BEHIND)
-                        old_chunk = x_pool.tile([P, chunk_k], BF16)
-                        nc.sync.dma_start(out=old_chunk[:], in_=state_x[:, first_k : first_k + chunk_k])
-                        old_chunks.append(old_chunk)
-                        move_scales(MOVES_BEHIND)
-                    wr_chunk = wr_pool.tile([P, CHUNK, N_TILE], U32, align_bytes=64)
-                    nc.sync.dma_start(
-                        out=wr_chunk[:].bitcast(I32),
-                        in_=w_receptance_words[c * CHUNK : (c + 1) * CHUNK]
-                        .rearrange("g p n t -> p g (n t)")
-                        .bitcast(I32),
-                    )
-                    wr_chunks.append(wr_chunk)
-                    move_scales(MOVES_BEHIND)
-                    if c < QUADRANTS:
-                        stage_output_scales(c)
+                for c, passes in enumerate(X_PASSES):
+                    first_pass = X_FIRST[c]
+                    cols = slice(first_pass * K_PASS, (first_pass + passes) * K_PASS)
+                    x_chunk = x_pool.tile([P, passes * K_PASS], BF16, name=f"x_{c}")
+                    nc.sync.dma_start(out=x_chunk[:], in_=x[:, cols])
+                    x_chunks.append(x_chunk)
+                    if c == 0:
+                        nc.sync.dma_start(
+                            out=mix_rows[0:PASSES, :].bitcast(BF16),
+                            in_=time_mix_r.rearrange("o (g k) -> (o g) k", k=K_PASS),
+                        )
+                    elif c == 1:
+                        move_scales(QUADRANTS)
+                    else:
+                        move_scales(MOVES_BEHIND_X)
+                    old_chunk = x_pool.tile([P, passes * K_PASS], BF16, name=f"old_{c}")
+                    nc.sync.dma_start(out=old_chunk[:], in_=state_x[:, cols])
+                    old_chunks.append(old_chunk)
+                    if c == 0:
+                        stage_receptance_scales()
+                    else:
+                        move_scales(2 * MOVES_BEHIND_X - QUADRANTS if c == 1 else MOVES_BEHIND_X)
+                    for w in range(first_pass // CHUNK, (first_pass + passes) // CHUNK):
+                        wr_chunk = wr_pool.tile([P, CHUNK, N_TILE], U32, align_bytes=64)
+                        nc.sync.dma_start(
+                            out=wr_chunk[:].bitcast(I32),
+                            in_=w_receptance_words[w * CHUNK : (w + 1) * CHUNK]
+                            .rearrange("g p n t -> p g (n t)")
+                            .bitcast(I32),
+                        )
+                        wr_chunks.append(wr_chunk)
+                        if c > 0:
+                            move_scales(MOVES_BEHIND_W)
+                            if w <= QUADRANTS:
+                                stage_output_scales(w - 1)
                 wo_bytes = w_output_words[0].rearrange("p n t -> p (n t)")
                 for c in range(OUT_CHUNKS):
                     wo_chunk = wo_pool.tile([P, out_cols], U32, align_bytes=64)
@@ -185,7 +198,7 @@ def tile_rwkv_timemix_for_quant_pb_k_kernel(
                         in_=wo_bytes[:, c * out_cols * PACK : (c + 1) * out_cols * PACK].bitcast(I32),
                     )
                     wo_chunks.append(wo_chunk)
-                    move_scales(QUADRANTS + len(moves) % QUADRANTS)
+                    move_scales(QUADRANTS)
 
                 inverse = work.tile([P, HIDDEN], F32)
                 nc.vector.reciprocal(out=inverse[:], in_=den[:])
@@ -214,7 +227,8 @@ def tile_rwkv_timemix_for_quant_pb_k_kernel(
                 acc = acc_pool.tile([P, HIDDEN], F32)
 
                 def turn(r):
-                    c, first = divmod(r * ROUND, X_CHUNK)
+                    c = max(i for i, first_pass in enumerate(X_FIRST) if first_pass <= r * ROUND)
+                    first = r * ROUND - X_FIRST[c]
                     x_words = x_chunks[c][:].bitcast(F32)
                     old_words = old_chunks[c][:].bitcast(F32)
                     x_turned = turned_pool.tile([P, ROUND, PAIR, P], F32)
@@ -321,18 +335,20 @@ def tile_rwkv_timemix_for_quant_pb_k_kernel(
 
         with (
             tc.psum_pool(name="bank", bufs=8) as bank_pool,
-            tc.tile_pool(name="result", bufs=OUT_CHUNKS) as result_pool,
+            tc.tile_pool(name="result", bufs=1) as result_pool,
         ):
-            for c in range(OUT_CHUNKS):
-                result = result_pool.tile([P, OUT_CHUNK, N_TILE], F32)
-                for v in range(OUT_CHUNK):
-                    j = c * OUT_CHUNK + v
+            stored = 0
+            for tiles in STORE_TILES:
+                result = result_pool.tile([P, tiles, N_TILE], F32, name=f"result_{stored}")
+                for v in range(tiles):
+                    j = stored + v
+                    c, w = divmod(j, OUT_CHUNK)
                     bank = bank_pool.tile([P, N_TILE], F32)
                     nc.tensor.matmul_mx(
                         out=bank[:],
                         lhsT=h_codes[:].bitcast(FP8X4),
                         lhsT_scale=h_scales[:],
-                        rhs=wo_chunks[c][:, v * N_TILE : (v + 1) * N_TILE].bitcast(FP8X4),
+                        rhs=wo_chunks[c][:, w * N_TILE : (w + 1) * N_TILE].bitcast(FP8X4),
                         rhs_scale=scale_plane(
                             wo_planes,
                             j // SPAN % SHARED,
@@ -346,6 +362,7 @@ def tile_rwkv_timemix_for_quant_pb_k_kernel(
                     else:
                         nc.vector.tensor_copy(out=result[:, v, :], in_=bank[:])
                 nc.sync.dma_start(
-                    out=out[:, c * out_cols : (c + 1) * out_cols],
+                    out=out[:, stored * N_TILE : (stored + tiles) * N_TILE],
                     in_=result[:].rearrange("p v n -> p (v n)"),
                 )
+                stored += tiles

@@ -35,18 +35,16 @@ QUADRANTS = SCALE_ROWS // PACK
 MOVED = PACK * SHARED
 SPAN = 2
 MOVE_ORDER = (0, 2, 1, 3)
-MOVES_BEHIND_X = 3
-MOVES_BEHIND_W = 2
 AHEAD = 2
 PASS_WORDS = K_PASS // PAIR
-
-assert CHUNK == SHARED
 
 FLOPS = 2 * 2 * P * EMBED * HIDDEN
 
 
-def scale_plane(planes, i, block):
-    return planes[PACK * i : P, block, :]
+def scale_plane(planes, j):
+    span, b = divmod(j, SPAN)
+    y, i = divmod(span, SHARED)
+    return planes[PACK * i : P, SPAN * y + b, :]
 
 
 def tile_rwkv_timemix_for_quant_pb_k_kernel(
@@ -105,54 +103,49 @@ def tile_rwkv_timemix_for_quant_pb_k_kernel(
                 nc.sync.dma_start(out=num[:], in_=wkv_num)
                 x_chunks, old_chunks, wr_chunks, wo_chunks = [], [], [], []
 
-                wr_staged = keep.tile([P, QUADRANTS, N_TILE], U8, align_bytes=64)
+                wr_staged = keep.tile([P, QUADRANTS // 2, SPAN, N_TILE], U8, align_bytes=64)
+                wo_staged = keep.tile([P, QUADRANTS // 2, SPAN, N_TILE], U8, align_bytes=64)
+                receptance_spans = w_receptance_scales.rearrange("(s b) q n -> b s q n", b=SPAN)
 
-                def stage_receptance_scales():
+                def stage_receptance_scales(b):
                     for quadrant in range(QUADRANTS):
+                        half = P // 2 * (quadrant % 2)
                         nc.sync.dma_start(
-                            out=wr_staged[:, quadrant, :].bitcast(I32),
-                            in_=w_receptance_scales[
-                                :, PACK * quadrant : PACK * (quadrant + 1), :
-                            ].bitcast(I32),
+                            out=wr_staged[half : half + P // 2, quadrant // 2, b, :].bitcast(I32),
+                            in_=receptance_spans[b, :, PACK * quadrant : PACK * (quadrant + 1), :].bitcast(I32),
                         )
 
-                wo_staged = keep.tile([P, QUADRANTS // 2, SPAN * N_TILE], U8, align_bytes=64)
-
-                def stage_output_scales(quadrant):
-                    half = P // 2 * (quadrant % 2)
-                    nc.sync.dma_start(
-                        out=wo_staged[half : half + P // 2, quadrant // 2, :].bitcast(I32),
-                        in_=w_output_scales[0, PACK * quadrant : PACK * (quadrant + 1), :]
-                        .rearrange("r (s m) -> s r m", m=SPAN * N_TILE)
-                        .bitcast(I32),
-                    )
-
-                moves = []
-                for c in range(CHUNKS):
-                    for quadrant in MOVE_ORDER:
-                        first = 32 * quadrant
-                        moves.append(
-                            (
-                                wr_planes[first : first + MOVED, c, :],
-                                wr_staged[MOVED * c : MOVED * (c + 1), quadrant, :],
-                            )
+                def stage_output_scales(quadrants):
+                    for quadrant in quadrants:
+                        half = P // 2 * (quadrant % 2)
+                        nc.sync.dma_start(
+                            out=wo_staged[half : half + P // 2, quadrant // 2, :, :]
+                            .rearrange("p b n -> p (b n)")
+                            .bitcast(I32),
+                            in_=w_output_scales[0, PACK * quadrant : PACK * (quadrant + 1), :]
+                            .rearrange("r (s m) -> s r m", m=SPAN * N_TILE)
+                            .bitcast(I32),
                         )
-                for y in range(BLOCKS // SPAN):
-                    for quadrant in MOVE_ORDER:
-                        first = 32 * quadrant
-                        source = P // 2 * (quadrant % 2) + MOVED * y
-                        moves.append(
-                            (
-                                wo_planes[first : first + MOVED, SPAN * y : SPAN * (y + 1), :].rearrange(
-                                    "p j n -> p (j n)"
-                                ),
-                                wo_staged[source : source + MOVED, quadrant // 2, :],
-                            )
-                        )
+
+                moves = [
+                    (planes, staged, y, quadrant)
+                    for planes, staged in ((wr_planes, wr_staged), (wo_planes, wo_staged))
+                    for y in range(BLOCKS // SPAN)
+                    for quadrant in MOVE_ORDER
+                ]
 
                 def move_scales(count):
-                    for target, source in moves[:count]:
-                        nc.sync.dma_start(out=target.bitcast(I32), in_=source.bitcast(I32))
+                    for planes, staged, y, quadrant in moves[:count]:
+                        target = 32 * quadrant
+                        source = P // 2 * (quadrant % 2) + MOVED * y
+                        nc.sync.dma_start(
+                            out=planes[target : target + MOVED, SPAN * y : SPAN * (y + 1), :]
+                            .rearrange("p j n -> p (j n)")
+                            .bitcast(I32),
+                            in_=staged[source : source + MOVED, quadrant // 2, :, :]
+                            .rearrange("p b n -> p (b n)")
+                            .bitcast(I32),
+                        )
                     moves[:count] = []
 
                 for c, passes in enumerate(X_PASSES):
@@ -166,17 +159,17 @@ def tile_rwkv_timemix_for_quant_pb_k_kernel(
                             out=mix_rows[0:PASSES, :].bitcast(BF16),
                             in_=time_mix_r.rearrange("o (g k) -> (o g) k", k=K_PASS),
                         )
-                    elif c == 1:
-                        move_scales(QUADRANTS)
-                    else:
-                        move_scales(MOVES_BEHIND_X)
+                    elif c > 1:
+                        move_scales(1)
                     old_chunk = x_pool.tile([P, passes * K_PASS], BF16, name=f"old_{c}")
                     nc.sync.dma_start(out=old_chunk[:], in_=state_x[:, cols])
                     old_chunks.append(old_chunk)
                     if c == 0:
-                        stage_receptance_scales()
+                        stage_receptance_scales(0)
+                    elif c == 1:
+                        move_scales(QUADRANTS)
                     else:
-                        move_scales(2 * MOVES_BEHIND_X - QUADRANTS if c == 1 else MOVES_BEHIND_X)
+                        move_scales(1)
                     for w in range(first_pass // CHUNK, (first_pass + passes) // CHUNK):
                         wr_chunk = wr_pool.tile([P, CHUNK, N_TILE], U32, align_bytes=64)
                         nc.sync.dma_start(
@@ -186,10 +179,14 @@ def tile_rwkv_timemix_for_quant_pb_k_kernel(
                             .bitcast(I32),
                         )
                         wr_chunks.append(wr_chunk)
-                        if c > 0:
-                            move_scales(MOVES_BEHIND_W)
-                            if w <= QUADRANTS:
-                                stage_output_scales(w - 1)
+                        if c == 0:
+                            stage_receptance_scales(1)
+                        elif c == 1:
+                            move_scales(QUADRANTS // 2)
+                        else:
+                            move_scales(1)
+                        if c == 2:
+                            stage_output_scales((0, 1) if w == first_pass // CHUNK else (2, 3))
                 wo_bytes = w_output_words[0].rearrange("p n t -> p (n t)")
                 for c in range(OUT_CHUNKS):
                     wo_chunk = wo_pool.tile([P, out_cols], U32, align_bytes=64)
@@ -293,7 +290,7 @@ def tile_rwkv_timemix_for_quant_pb_k_kernel(
                             lhsT=xr_codes[:, rows].bitcast(FP8X4),
                             lhsT_scale=xr_scales[:, rows],
                             rhs=wr_chunks[g // CHUNK][:, g % CHUNK, :].bitcast(FP8X4),
-                            rhs_scale=scale_plane(wr_planes, g % CHUNK, g // CHUNK),
+                            rhs_scale=scale_plane(wr_planes, g),
                             start=(g == 0),
                             stop=(g == PASSES - 1),
                         )
@@ -349,11 +346,7 @@ def tile_rwkv_timemix_for_quant_pb_k_kernel(
                         lhsT=h_codes[:].bitcast(FP8X4),
                         lhsT_scale=h_scales[:],
                         rhs=wo_chunks[c][:, w * N_TILE : (w + 1) * N_TILE].bitcast(FP8X4),
-                        rhs_scale=scale_plane(
-                            wo_planes,
-                            j // SPAN % SHARED,
-                            j // (SPAN * SHARED) * SPAN + j % SPAN,
-                        ),
+                        rhs_scale=scale_plane(wo_planes, j),
                         start=True,
                         stop=True,
                     )

import concourse.mybir as mybir
from concourse.masks import make_identity

F32 = mybir.dt.float32
BF16 = mybir.dt.bfloat16
U8 = mybir.dt.uint8
U32 = mybir.dt.uint32
I32 = mybir.dt.int32
FP8X4 = mybir.dt.float8_e4m3fn_x4
ALU = mybir.AluOpType
ACT = mybir.ActivationFunctionType

P = 128
PACK = 4
PAIR = 2
K_PASS = P * PACK
EMBED = 16384
HIDDEN = 512
N_TILE = 512
PASSES = EMBED // K_PASS
OUT_TILES = EMBED // N_TILE
CHUNK = 4
CHUNKS = PASSES // CHUNK
X_PASSES = (4, 8, 8, 12)
X_FIRST = (0, 4, 12, 20)
OUT_CHUNK = 8
OUT_CHUNKS = OUT_TILES // OUT_CHUNK
STORE_TILES = (4, 4, 8, 8, 8)
ROUND = 2
SCALE_ROWS = 16
SHARED = 4
BLOCKS = PASSES // SHARED
ROUNDS = PASSES // ROUND
QUADRANTS = SCALE_ROWS // PACK
MOVED = PACK * SHARED
SPAN = 2
MOVE_ORDER = (0, 2, 1, 3)
AHEAD = 2
PASS_WORDS = K_PASS // PAIR

FLOPS = 2 * 2 * P * EMBED * HIDDEN


def scale_plane(planes, j):
    span, b = divmod(j, SPAN)
    y, i = divmod(span, SHARED)
    return planes[PACK * i : P, SPAN * y + b, :]


def tile_rwkv_timemix_for_quant_pb_k_kernel(
    tc,
    x,
    state_x,
    time_mix_r,
    w_receptance_words,
    w_receptance_scales,
    wkv_num,
    wkv_den,
    w_output_words,
    w_output_scales,
    out,
):
    nc = tc.nc
    out_cols = OUT_CHUNK * N_TILE

    with (
        tc.manual_schedule(),
        tc.tile_pool(name="keep", bufs=1) as keep,
        tc.tile_pool(name="wo", bufs=OUT_CHUNKS) as wo_pool,
    ):
        identity = keep.tile([P, P], F32)
        make_identity(nc, identity[:])

        mix_rows = keep.tile([P, PASS_WORDS], F32)
        nc.vector.memset(mix_rows[:], 0.0)

        first_column = keep.tile([P, 2], F32)
        nc.vector.memset(first_column[:], 0.0)
        nc.scalar.activation(out=first_column[:, 1:2], in_=first_column[:, 0:1], func=ACT.Copy, scale=1.0)

        wr_planes = keep.tile([P, BLOCKS, N_TILE], U8, align_bytes=64)
        wo_planes = keep.tile([P, BLOCKS, N_TILE], U8, align_bytes=64)
        nc.vector.memset(wr_planes[:].rearrange("p j n -> p (j n)").bitcast(I32), 0)
        nc.vector.memset(wo_planes[:].rearrange("p j n -> p (j n)").bitcast(I32), 0)

        num = keep.tile([P, HIDDEN], BF16)
        den = keep.tile([P, HIDDEN], BF16)
        ratio = keep.tile([P, PACK, P], F32)
        h_codes = keep.tile([P, P], U32, align_bytes=64)
        h_scales = keep.tile([P, P], U8, align_bytes=64)

        with (
            tc.psum_pool(name="acc", bufs=1) as acc_pool,
            tc.psum_pool(name="turned", bufs=AHEAD + 1) as turned_pool,
            tc.psum_pool(name="small", bufs=1) as small_pool,
        ):
            with (
                tc.tile_pool(name="x", bufs=1) as x_pool,
                tc.tile_pool(name="wr", bufs=CHUNKS) as wr_pool,
                tc.tile_pool(name="work", bufs=2) as work,
            ):
                nc.sync.dma_start(out=den[:], in_=wkv_den)
                nc.sync.dma_start(out=num[:], in_=wkv_num)
                x_chunks, old_chunks, wr_chunks, wo_chunks = [], [], [], []

                wr_staged = keep.tile([P, QUADRANTS // 2, SPAN, N_TILE], U8, align_bytes=64)
                wo_staged = keep.tile([P, QUADRANTS // 2, SPAN, N_TILE], U8, align_bytes=64)
                receptance_spans = w_receptance_scales.rearrange("(s b) q n -> b s q n", b=SPAN)

                def stage_receptance_scales(b):
                    for quadrant in range(QUADRANTS):
                        half = P // 2 * (quadrant % 2)
                        nc.sync.dma_start(
                            out=wr_staged[half : half + P // 2, quadrant // 2, b, :].bitcast(I32),
                            in_=receptance_spans[b, :, PACK * quadrant : PACK * (quadrant + 1), :].bitcast(I32),
                        )

                def stage_output_scales(quadrants):
                    for quadrant in quadrants:
                        half = P // 2 * (quadrant % 2)
                        nc.sync.dma_start(
                            out=wo_staged[half : half + P // 2, quadrant // 2, :, :]
                            .rearrange("p b n -> p (b n)")
                            .bitcast(I32),
                            in_=w_output_scales[0, PACK * quadrant : PACK * (quadrant + 1), :]
                            .rearrange("r (s m) -> s r m", m=SPAN * N_TILE)
                            .bitcast(I32),
                        )

                moves = [
                    (planes, staged, y, quadrant)
                    for planes, staged in ((wr_planes, wr_staged), (wo_planes, wo_staged))
                    for y in range(BLOCKS // SPAN)
                    for quadrant in MOVE_ORDER
                ]

                def move_scales(count):
                    for planes, staged, y, quadrant in moves[:count]:
                        target = 32 * quadrant
                        source = P // 2 * (quadrant % 2) + MOVED * y
                        nc.sync.dma_start(
                            out=planes[target : target + MOVED, SPAN * y : SPAN * (y + 1), :]
                            .rearrange("p j n -> p (j n)")
                            .bitcast(I32),
                            in_=staged[source : source + MOVED, quadrant // 2, :, :]
                            .rearrange("p b n -> p (b n)")
                            .bitcast(I32),
                        )
                    moves[:count] = []

                for c, passes in enumerate(X_PASSES):
                    first_pass = X_FIRST[c]
                    cols = slice(first_pass * K_PASS, (first_pass + passes) * K_PASS)
                    x_chunk = x_pool.tile([P, passes * K_PASS], BF16, name=f"x_{c}")
                    nc.sync.dma_start(out=x_chunk[:], in_=x[:, cols])
                    x_chunks.append(x_chunk)
                    if c == 0:
                        nc.sync.dma_start(
                            out=mix_rows[0:PASSES, :].bitcast(BF16),
                            in_=time_mix_r.rearrange("o (g k) -> (o g) k", k=K_PASS),
                        )
                    elif c > 1:
                        move_scales(1)
                    old_chunk = x_pool.tile([P, passes * K_PASS], BF16, name=f"old_{c}")
                    nc.sync.dma_start(out=old_chunk[:], in_=state_x[:, cols])
                    old_chunks.append(old_chunk)
                    if c == 0:
                        stage_receptance_scales(0)
                    elif c == 1:
                        move_scales(QUADRANTS)
                    else:
                        move_scales(1)
                    for w in range(first_pass // CHUNK, (first_pass + passes) // CHUNK):
                        wr_chunk = wr_pool.tile([P, CHUNK, N_TILE], U32, align_bytes=64)
                        nc.sync.dma_start(
                            out=wr_chunk[:].bitcast(I32),
                            in_=w_receptance_words[w * CHUNK : (w + 1) * CHUNK]
                            .rearrange("g p n t -> p g (n t)")
                            .bitcast(I32),
                        )
                        wr_chunks.append(wr_chunk)
                        if c == 0:
                            stage_receptance_scales(1)
                        elif c == 1:
                            move_scales(QUADRANTS // 2)
                        else:
                            move_scales(1)
                        if c == 2:
                            stage_output_scales((0, 1) if w == first_pass // CHUNK else (2, 3))
                wo_bytes = w_output_words[0].rearrange("p n t -> p (n t)")
                for c in range(OUT_CHUNKS):
                    wo_chunk = wo_pool.tile([P, out_cols], U32, align_bytes=64)
                    nc.sync.dma_start(
                        out=wo_chunk[:].bitcast(I32),
                        in_=wo_bytes[:, c * out_cols * PACK : (c + 1) * out_cols * PACK].bitcast(I32),
                    )
                    wo_chunks.append(wo_chunk)
                    move_scales(QUADRANTS)

                inverse = work.tile([P, HIDDEN], F32)
                nc.vector.reciprocal(out=inverse[:], in_=den[:])
                nc.vector.tensor_tensor(
                    out=ratio[:],
                    in0=num[:].rearrange("b (p t) -> b t p", t=PACK),
                    in1=inverse[:].rearrange("b (p t) -> b t p", t=PACK),
                    op=ALU.mult,
                )

                mix_turned = small_pool.tile([P, PAIR, P], F32, tag="small")
                for u in range(PAIR):
                    nc.tensor.transpose(mix_turned[:, u, :], mix_rows[:, u:PASS_WORDS:PAIR], identity[:])
                take_new = keep.tile([P, PASSES * PACK], F32)
                keep_old = keep.tile([P, PASSES * PACK], F32)
                nc.vector.tensor_copy(
                    out=take_new[:].rearrange("p (g u e) -> p g u e", u=PAIR, e=PAIR),
                    in_=mix_turned[:]
                    .bitcast(BF16)
                    .rearrange("p u (g e) -> p g u e", e=PAIR)[:, 0:PASSES, :, :],
                )
                nc.vector.tensor_scalar(
                    out=keep_old[:], in0=take_new[:], scalar1=-1.0, scalar2=1.0, op0=ALU.mult, op1=ALU.add
                )

                acc = acc_pool.tile([P, HIDDEN], F32)

                def turn(r):
                    c = max(i for i, first_pass in enumerate(X_FIRST) if first_pass <= r * ROUND)
                    first = r * ROUND - X_FIRST[c]
                    x_words = x_chunks[c][:].bitcast(F32)
                    old_words = old_chunks[c][:].bitcast(F32)
                    x_turned = turned_pool.tile([P, ROUND, PAIR, P], F32)
                    old_turned = turned_pool.tile([P, ROUND, PAIR, P], F32)
                    for s in range(ROUND):
                        for u in range(PAIR):
                            cols = slice((first + s) * PASS_WORDS + u, (first + s + 1) * PASS_WORDS, PAIR)
                            nc.tensor.transpose(x_turned[:, s, u, :], x_words[:, cols], identity[:])
                            nc.tensor.transpose(old_turned[:, s, u, :], old_words[:, cols], identity[:])
                    return x_turned, old_turned

                def mix(r, x_turned, old_turned):
                    x_pairs = x_turned[:].bitcast(BF16).rearrange("p s u (b e) -> p s u b e", e=PAIR)
                    old_pairs = old_turned[:].bitcast(BF16).rearrange("p s u (b e) -> p s u b e", e=PAIR)
                    old_part = work.tile([P, ROUND, PACK, P], F32)
                    mixed = work.tile([P, ROUND, PACK, P], BF16)
                    for s in range(ROUND):
                        for t in range(PACK):
                            u, e = divmod(t, PAIR)
                            col = (r * ROUND + s) * PACK + t
                            nc.scalar.activation(
                                out=old_part[:, s, t, :],
                                in_=old_pairs[:, s, u, :, e],
                                func=ACT.Copy,
                                scale=keep_old[:, col : col + 1],
                            )
                            nc.vector.scalar_tensor_tensor(
                                out=mixed[:, s, t, :],
                                in0=x_pairs[:, s, u, :, e],
                                scalar=take_new[:, col : col + 1],
                                in1=old_part[:, s, t, :],
                                op0=ALU.mult,
                                op1=ALU.add,
                            )
                    return mixed

                def regroup(mixed):
                    grouped = work.tile([P, ROUND, P, PACK], BF16, align_bytes=64)
                    nc.gpsimd.tensor_scalar(
                        out=grouped[:],
                        in0=mixed[:].rearrange("p s t b -> p s b t"),
                        scalar1=1.0,
                        scalar2=0.0,
                        op0=ALU.mult,
                        op1=ALU.add,
                    )
                    return grouped

                def quantise_and_multiply(r, grouped):
                    xr_codes = work.tile([P, ROUND * P], U32, align_bytes=64)
                    xr_scales = work.tile([P, ROUND * P], U8, align_bytes=64)
                    nc.vector.quantize_mx(
                        out=xr_codes[:].bitcast(FP8X4),
                        scales=xr_scales[:],
                        in_=grouped[:].rearrange("p s b t -> p (s b t)"),
                    )
                    for s in range(ROUND):
                        g = r * ROUND + s
                        rows = slice(s * P, (s + 1) * P)
                        nc.tensor.matmul_mx(
                            out=acc[:],
                            lhsT=xr_codes[:, rows].bitcast(FP8X4),
                            lhsT_scale=xr_scales[:, rows],
                            rhs=wr_chunks[g // CHUNK][:, g % CHUNK, :].bitcast(FP8X4),
                            rhs_scale=scale_plane(wr_planes, g),
                            start=(g == 0),
                            stop=(g == PASSES - 1),
                        )

                turned = [turn(r) for r in range(AHEAD)]
                grouped = None
                for r in range(ROUNDS):
                    if r + AHEAD < ROUNDS:
                        turned.append(turn(r + AHEAD))
                    mixed = mix(r, turned[r][0], turned[r][1])
                    if r > 0:
                        quantise_and_multiply(r - 1, grouped)
                    grouped = regroup(mixed)
                quantise_and_multiply(ROUNDS - 1, grouped)

            with tc.tile_pool(name="gate", bufs=1) as gate_pool:
                lifted = gate_pool.tile([P, PACK, P], F32)
                nc.scalar.activation(
                    out=lifted[:],
                    in_=acc[:].rearrange("b (p t) -> b t p", t=PACK),
                    func=ACT.Relu,
                    scale=1.0 / 6.0,
                    bias=0.5,
                )
                h = gate_pool.tile([P, PACK, P], F32)
                nc.vector.scalar_tensor_tensor(
                    out=h[:], in0=lifted[:], scalar=1.0, in1=ratio[:], op0=ALU.min, op1=ALU.mult
                )
                h_turned = small_pool.tile([P, PACK, P], F32, tag="small")
                for t in range(PACK):
                    nc.tensor.transpose(h_turned[:, t, :], h[:, t, :], identity[:])
                h_grouped = gate_pool.tile([P, P, PACK], BF16, align_bytes=64)
                nc.vector.tensor_copy(out=h_grouped[:], in_=h_turned[:].rearrange("p t b -> p b t"))
                nc.vector.quantize_mx(
                    out=h_codes[:].bitcast(FP8X4),
                    scales=h_scales[:],
                    in_=h_grouped[:].rearrange("p b t -> p (b t)"),
                )

        with (
            tc.psum_pool(name="bank", bufs=8) as bank_pool,
            tc.tile_pool(name="result", bufs=1) as result_pool,
        ):
            stored = 0
            for tiles in STORE_TILES:
                result = result_pool.tile([P, tiles, N_TILE], F32, name=f"result_{stored}")
                for v in range(tiles):
                    j = stored + v
                    c, w = divmod(j, OUT_CHUNK)
                    bank = bank_pool.tile([P, N_TILE], F32)
                    nc.tensor.matmul_mx(
                        out=bank[:],
                        lhsT=h_codes[:].bitcast(FP8X4),
                        lhsT_scale=h_scales[:],
                        rhs=wo_chunks[c][:, w * N_TILE : (w + 1) * N_TILE].bitcast(FP8X4),
                        rhs_scale=scale_plane(wo_planes, j),
                        start=True,
                        stop=True,
                    )
                    if j % 2 == 0:
                        nc.scalar.copy(out=result[:, v, :], in_=bank[:])
                    else:
                        nc.vector.tensor_copy(out=result[:, v, :], in_=bank[:])
                nc.sync.dma_start(
                    out=out[:, stored * N_TILE : (stored + tiles) * N_TILE],
                    in_=result[:].rearrange("p v n -> p (v n)"),
                )
                stored += tiles
